import numpy as np
import ml_dtypes


def mxq(x, axis, fmt="e4m3"):
    dtype, down = {"e4m3": (ml_dtypes.float8_e4m3fn, 7), "e5m2": (ml_dtypes.float8_e5m2, 14)}[fmt]
    v = np.moveaxis(np.asarray(x, np.float32).astype(ml_dtypes.bfloat16).astype(np.float64), axis, -1)
    blocks = v.reshape(v.shape[:-1] + (-1, 32))
    amax = np.abs(blocks).max(-1, keepdims=True)
    byte = np.maximum(np.where(amax > 0, np.frexp(amax)[1] - 1 + 127, 0) - down, 1)
    scale = np.exp2(byte - 127.0)
    codes = (blocks / scale).astype(np.float32).astype(dtype).astype(np.float64)
    return np.moveaxis((codes * scale).reshape(v.shape), -1, axis)


WIDE = False


def mx_kscale(k):
    if not WIDE:
        return np.ones(k)
    levels = np.array([10, -10, 5, -5, 0])
    a = np.random.permutation(np.resize(levels, k // 512 * 4)).reshape(k // 512, 4)
    idx = np.arange(k)
    return np.exp2(a[idx // 512, idx % 128 // 32])


BF16 = ml_dtypes.bfloat16


def bf(x):
    return np.asarray(x, np.float32).astype(BF16)


def f64(x):
    return np.asarray(x).astype(np.float64)


B, N, L, M, F = 8, 32, 512, 128, 64
EPS = 1e-8
KAPPA0 = -3.0


def softplus(v):
    return np.logaddexp(v, 0.0)


def sigmoid(v):
    return 1.0 / (1.0 + np.exp(-v))


def setup_inputs():
    e = np.log2(mx_kscale(L))
    keep = np.abs(e) == np.abs(e).min()
    k0 = softplus(KAPPA0)
    t = np.zeros(L)
    t[keep] = np.sort(np.random.uniform(0.0, 1.0, int(keep.sum())))
    off = k0 * (np.log(2.0) * 2.0 * np.abs(e) + np.random.uniform(0.0, 1.0, L))
    t = np.where(keep, t, np.where(e > 0, 1.0 + off, -off))[:, None]
    t_left = np.random.uniform(0.0, 1.0, (N, M)) * 0.8
    t_right = t_left + 0.05 + 0.15 * np.random.uniform(0.0, 1.0, (N, M))
    kappa = KAPPA0 + 0.3 * np.random.standard_normal((N, 1))
    tq = f64(bf(t))[:, 0]
    kq = softplus(f64(bf(kappa)))
    d = np.maximum(np.maximum(tq - 1.0, -tq), 0.0)
    g = np.where(d > 0.0, 0.5, 1.0) * np.exp(d[None, :] / kq)
    x_aug = np.random.standard_normal((B, N, L, F)) * 0.15 * np.sqrt(L) * g[None, :, :, None]
    return {"x_aug": bf(x_aug), "t": bf(t), "t_left": bf(t_left), "t_right": bf(t_right), "kappa": bf(kappa)}


def reference(x_aug, t, t_left, t_right, kappa):
    t = f64(t)
    k = softplus(f64(kappa))[None, :, None]
    tl = f64(t_left)[None, :, None, :]
    tr = f64(t_right)[None, :, None, :]
    alpha = sigmoid((tr - t) / k) * sigmoid((t - tl) / k)
    numerator = mxq(alpha[0], 1, "e4m3").transpose(0, 2, 1) @ mxq(f64(x_aug), 2, "e4m3")
    denominator = alpha.sum(axis=2)[..., None]
    return numerator / (denominator + EPS)

@@ -1,0 +1,391 @@
+from contextlib import ExitStack
+
+import concourse.mybir as mybir
+from concourse.masks import make_identity
+
+F32 = mybir.dt.float32
+BF16 = mybir.dt.bfloat16
+U32 = mybir.dt.uint32
+I32 = mybir.dt.int32
+U8 = mybir.dt.uint8
+FP8X4 = mybir.dt.float8_e4m3fn_x4
+ACT = mybir.ActivationFunctionType
+ALU = mybir.AluOpType
+
+B = 8
+N = 32
+L = 512
+M = 128
+F = 64
+EPS = 1e-8
+P = 128
+PAIRS = N // 2
+FLOPS = 2 * B * N * M * F * L
+
+XRAW_BUFS = 24
+A_SLOTS = 8
+TILES = 32
+PRELOAD = 12
+X_SKIP = (6, 12, 18, 24, 30)
+S_TILE = 6
+S_TILE_STEP = 2
+BIASES = (2.0, 1.0, 1.0 / 5.0, 1.0 / 9.0, 1.0 / 13.0)
+SLOPES = (1.0 / 3.0, 1.0 / 7.0, 1.0 / 11.0, 1.0 / 15.0)
+
+
+def tile_weightedaggregation_kernel(tc, x_aug, t, t_left, t_right, kappa, out):
+    nc = tc.nc
+    xv = x_aug.rearrange("b n (p j) f -> n p b (j f)", j=4)
+    ov = out.rearrange("b (h nl) (mh ml) f -> h (nl mh) b (ml f)", nl=2, ml=2)
+
+    with ExitStack() as ctx:
+        const = ctx.enter_context(tc.tile_pool(name="const", bufs=1))
+        xraw = ctx.enter_context(tc.tile_pool(name="xraw", bufs=XRAW_BUFS))
+        xgrp = ctx.enter_context(tc.tile_pool(name="xgrp", bufs=4))
+        xq = ctx.enter_context(tc.tile_pool(name="xq", bufs=10))
+        sig = ctx.enter_context(tc.tile_pool(name="sig", bufs=4))
+        apool = ctx.enter_context(tc.tile_pool(name="apool", bufs=4))
+        small = ctx.enter_context(tc.tile_pool(name="small", bufs=4))
+        opool = ctx.enter_context(tc.tile_pool(name="opool", bufs=5))
+        ps_a = ctx.enter_context(tc.psum_pool(name="ps_a", bufs=4))
+        ps_o = ctx.enter_context(tc.psum_pool(name="ps_o", bufs=4))
+        ctx.enter_context(tc.manual_schedule())
+
+        x_tiles = {}
+        xg_tiles = {}
+        xq_tiles = {}
+        sig_tiles = {}
+        a32_tiles = {}
+        den_tiles = {}
+        rec_tiles = {}
+        at_tiles = {}
+        ain_tiles = {}
+        acc_tiles = {}
+        osb_tiles = {}
+
+        def load_x(n):
+            xr = xraw.tile([P, B, 4 * F], BF16, name="xr")
+            nc.sync.dma_start(out=xr[:, 0:4, :], in_=xv[n][:, 0:4, :])
+            nc.sync.dma_start(out=xr[:, 4:8, :], in_=xv[n][:, 4:8, :])
+            x_tiles[n] = xr
+
+        def x_regroup(n, halves):
+            xr = x_tiles[n]
+            xg = xgrp.tile([P, 4 * B * F], BF16, name="xg", align_bytes=64)
+            dst = xg[:].rearrange("p (b c i j) -> p b c j i", b=B, c=16, i=4, j=4)
+            src = xr[:].rearrange("p b (j c i) -> p b c j i", j=4, c=16, i=4)
+            if halves:
+                nc.vector.tensor_copy(out=dst[:, 0:4], in_=src[:, 0:4])
+                nc.vector.tensor_copy(out=dst[:, 4:8], in_=src[:, 4:8])
+            else:
+                nc.vector.tensor_copy(out=dst, in_=src)
+            xg_tiles[n] = xg
+
+        def x_regroup_scalar(n):
+            xg = xgrp.tile([P, 4 * B * F], BF16, name="xg", align_bytes=64)
+            nc.scalar.copy(
+                out=xg[:].rearrange("p (b f j) -> p b f j", b=B, f=F, j=4),
+                in_=x_tiles[n][:].rearrange("p b (j f) -> p b f j", j=4),
+            )
+            xg_tiles[n] = xg
+
+        def x_quant(n, halves):
+            xg = xg_tiles[n]
+            xc = xq.tile([P, B * F], U32, name="xc", align_bytes=64)
+            xp = xq.tile([P, B * F], U8, name="xp", align_bytes=64)
+            if halves:
+                for bh in range(2):
+                    nc.vector.quantize_mx(
+                        out=xc[:, 256 * bh : 256 * bh + 256].bitcast(FP8X4),
+                        scales=xp[:, 256 * bh : 256 * bh + 256],
+                        in_=xg[:, 1024 * bh : 1024 * bh + 1024],
+                    )
+            else:
+                nc.vector.quantize_mx(out=xc[:].bitcast(FP8X4), scales=xp[:], in_=xg[:])
+            xq_tiles[n] = (xc, xp)
+
+        kap = const.tile([P, 2], BF16, name="kap")
+        nc.vector.memset(kap[:], 0.0)
+        nc.scalar.dma_start(out=kap[0:16, :], in_=kappa.rearrange("(h l) o -> h (l o)", l=2))
+        t_row = const.tile([P, L], BF16, name="t_row")
+        nc.vector.memset(t_row[:], 0.0)
+        nc.scalar.dma_start(out=t_row[0:1, :], in_=t.rearrange("l o -> o l"))
+        raw = const.tile([P, 3, 2, M], BF16, name="raw")
+        nc.vector.memset(raw[:, 0:2, :, :], 0.0)
+        nc.vector.memset(raw[:, 2, :, :], 1.0)
+        nc.scalar.dma_start(out=raw[0:16, 0, :, :], in_=t_right.rearrange("(h l) m -> h l m", l=2))
+        nc.scalar.dma_start(out=raw[0:16, 1, :, :], in_=t_left.rearrange("(h l) m -> h l m", l=2))
+        for n in range(PRELOAD):
+            load_x(n)
+
+        cb = const.tile([P, len(BIASES)], F32, name="cb")
+        for i in range(len(BIASES)):
+            nc.vector.memset(cb[:, i : i + 1], BIASES[i])
+        warm = const.tile([P, 1], F32, name="warm")
+        nc.scalar.activation(out=warm[:], in_=cb[:, 0:1], func=ACT.Sigmoid)
+
+        ident = const.tile([P, P], F32, name="ident")
+        make_identity(nc, ident[:])
+        ones_bf = const.tile([P, P], BF16, name="ones_bf")
+        nc.vector.memset(ones_bf[:], 1.0)
+        a_cod = []
+        a_pl = []
+        for s in range(A_SLOTS):
+            ac = const.tile([P, 4, 64], U32, name="a_cod%d" % s, align_bytes=64)
+            ap = const.tile([P, 4, 64], U8, name="a_pl%d" % s, align_bytes=64)
+            nc.vector.memset(ac[:, 0:4:3, :].bitcast(I32), 0)
+            nc.vector.memset(ap[:, 0:4:3, :].bitcast(I32), 0)
+            a_cod.append(ac[:].rearrange("p g c -> p (g c)"))
+            a_pl.append(ap[:].rearrange("p g c -> p (g c)"))
+        swp = const.tile([P, P], F32, name="swp")
+        nc.vector.tensor_copy(out=swp[:, 0:64], in_=ident[:, 64:128])
+        nc.vector.tensor_copy(out=swp[:, 64:128], in_=ident[:, 0:64])
+
+        t_ps = ps_a.tile([P, L], F32, name="t_ps", tag="at")
+        nc.tensor.matmul(t_ps[:], lhsT=ones_bf[:], rhs=t_row[:], start=True, stop=True)
+
+        def fma(out, in_, scale, bias):
+            nc.scalar.activation(out=out, in_=in_, func=ACT.Identity, scale=scale, bias=bias)
+
+        def col(tl, c):
+            return tl[:, c : c + 1]
+
+        k_u = const.tile([P, 2], F32, name="k_u")
+        nc.scalar.activation(out=k_u[:], in_=kap[:], func=ACT.Abs)
+        k_s = const.tile([P, 2], F32, name="k_s")
+        nc.scalar.activation(out=k_s[:], in_=k_u[:], func=ACT.Sigmoid, scale=-1.0)
+        k_d = const.tile([P, 2], F32, name="k_d")
+        fma(k_d[:], k_s[:], -1.0, col(cb, 0))
+        k_rl = const.tile([P, 2], F32, name="k_rl")
+        nc.scalar.activation(out=k_rl[:], in_=kap[:], func=ACT.Relu)
+
+        xg0 = xgrp.tile([P, 4 * B * F], BF16, name="xg", align_bytes=64)
+        xg_tiles[0] = xg0
+        dst0 = xg0[:].rearrange("p (b c i j) -> p b c j i", b=B, c=16, i=4, j=4)
+        src0 = x_tiles[0][:].rearrange("p b (j c i) -> p b c j i", j=4, c=16, i=4)
+        nc.vector.tensor_copy(out=dst0[:, 0:4], in_=src0[:, 0:4])
+        k_rd = const.tile([P, 2], F32, name="k_rd")
+        nc.vector.reciprocal(out=k_rd[:], in_=k_d[:])
+        nc.vector.tensor_copy(out=dst0[:, 4:8], in_=src0[:, 4:8])
+        t_perm = const.tile([P, 4, P], F32, name="t_perm")
+        nc.vector.tensor_copy(out=t_perm[:], in_=t_ps[:].rearrange("q (p j) -> q j p", j=4))
+        t_flat = t_perm[:].rearrange("q j p -> q (j p)")
+
+        k_z = const.tile([P, 2], F32, name="k_z")
+        for c in range(2):
+            nc.scalar.activation(out=col(k_z, c), in_=col(k_s, c), func=ACT.Copy, scale=col(k_rd, c))
+        k_z2 = const.tile([P, 2], F32, name="k_z2")
+        nc.scalar.activation(out=k_z2[:], in_=k_z[:], func=ACT.Square)
+        k_z4 = const.tile([P, 2], F32, name="k_z4")
+        nc.scalar.activation(out=k_z4[:], in_=k_z2[:], func=ACT.Square)
+        k_e = const.tile([P, 4, 2], F32, name="k_e")
+        for i in range(4):
+            fma(k_e[:, i, :], k_z2[:], SLOPES[i], col(cb, i + 1))
+        k_z8 = const.tile([P, 2], F32, name="k_z8")
+        nc.scalar.activation(out=k_z8[:], in_=k_z4[:], func=ACT.Square)
+        k_f = const.tile([P, 2, 2], F32, name="k_f")
+        for i in range(2):
+            for c in range(2):
+                fma(k_f[:, i, c : c + 1], k_e[:, 2 * i + 1, c : c + 1], col(k_z4, c), k_e[:, 2 * i, c : c + 1])
+        k_g = const.tile([P, 2], F32, name="k_g")
+        for c in range(2):
+            fma(col(k_g, c), k_f[:, 1, c : c + 1], col(k_z8, c), k_f[:, 0, c : c + 1])
+        k_w = const.tile([P, 2], F32, name="k_w")
+        for c in range(2):
+            nc.scalar.activation(out=col(k_w, c), in_=col(k_g, c), func=ACT.Copy, scale=col(k_z, c))
+
+        x_quant(0, False)
+
+        k_sp = const.tile([P, 2], F32, name="k_sp")
+        nc.vector.scalar_tensor_tensor(
+            out=k_sp[:], in0=k_w[:], scalar=2.0, in1=k_rl[:], op0=ALU.mult, op1=ALU.add
+        )
+        rk = const.tile([P, 2], F32, name="rk")
+        nc.vector.reciprocal(out=rk[:], in_=k_sp[:])
+        scaled = const.tile([P, 3, 2, M], F32, name="scaled")
+        for nl in range(2):
+            nc.scalar.activation(out=scaled[:, :, nl, :], in_=raw[:, :, nl, :], func=ACT.Copy,
+                                 scale=rk[:, nl : nl + 1])
+        sc_v = scaled[:].rearrange("r g l m -> r g (l m)").rearrange("r g (c e) -> r g e c", e=2)
+        tp_ps = ps_a.tile([P, 3, P], F32, name="tp_ps", tag="at")
+        tn_ps = ps_a.tile([P, 3, P], F32, name="tn_ps", tag="at")
+        for ml in range(2):
+            nc.tensor.transpose(tp_ps[:, ml, :], sc_v[:, 0, ml, :], ident[:])
+        nc.tensor.transpose(tp_ps[:, 2, :], sc_v[:, 2, 0, :], ident[:])
+        for ml in range(2):
+            nc.tensor.transpose(tn_ps[:, ml, :], sc_v[:, 1, ml, :], ident[:])
+        nc.tensor.transpose(tn_ps[:, 2, :], sc_v[:, 2, 0, :], ident[:])
+        tabp = const.tile([P, 3, 16], F32, name="tabp")
+        nc.scalar.copy(out=tabp[:], in_=tp_ps[:, :, 0:16])
+        tabn = const.tile([P, 3, 16], F32, name="tabn")
+        nc.scalar.activation(out=tabn[:], in_=tn_ps[:, :, 0:16], func=ACT.Copy, scale=-1.0)
+
+        x_regroup(1, False)
+        x_regroup(2, False)
+        x_quant(1, False)
+
+        def sigmoids(i):
+            h, ml = divmod(i, 2)
+            s1 = sig.tile([P, L], F32, name="s1")
+            nc.scalar.activation(out=s1[:], in_=t_flat, func=ACT.Sigmoid,
+                                 scale=tabn[:, 2, h : h + 1], bias=tabp[:, ml, h : h + 1])
+            s2 = sig.tile([P, L], F32, name="s2")
+            nc.scalar.activation(out=s2[:], in_=t_flat, func=ACT.Sigmoid,
+                                 scale=tabp[:, 2, h : h + 1], bias=tabn[:, ml, h : h + 1])
+            sig_tiles[i] = (s1, s2)
+
+        def product(i):
+            g, c = divmod(i, 4)
+            if c == 0:
+                den = small.tile([P, 4], F32, name="den")
+                den_tiles[g] = den
+            s1, s2 = sig_tiles[i]
+            a32 = apool.tile([P, L], F32, name="a32")
+            nc.vector.scalar_tensor_tensor(
+                out=a32[:], in0=s1[:], scalar=1.0, in1=s2[:],
+                op0=ALU.mult, op1=ALU.mult, accum_out=den_tiles[g][:, c : c + 1],
+            )
+            a32_tiles[i] = a32
+
+        dene_tiles = {}
+
+        def add_eps(g):
+            dene = small.tile([P, 4], F32, name="dene")
+            nc.vector.tensor_scalar_add(out=dene[:], in0=den_tiles[g][:], scalar1=EPS)
+            dene_tiles[g] = dene
+
+        def reciprocal(g):
+            rec = small.tile([P, 4], F32, name="rec")
+            nc.vector.reciprocal(out=rec[:], in_=dene_tiles[g][:])
+            rec_tiles[g] = rec
+
+        def transposes(i):
+            a32 = a32_tiles[i]
+            at = ps_a.tile([P, 4, P], F32, name="at", tag="at")
+            for j in range(4):
+                nc.tensor.transpose(at[:, j, :], a32[:, j * P : (j + 1) * P], swp[:])
+            at_tiles[i] = at
+
+        def alpha_out(i):
+            a_in = apool.tile([P, P, 4], BF16, name="a_in", align_bytes=64)
+            nc.scalar.copy(out=a_in[:], in_=at_tiles[i][:].rearrange("p j q -> p q j"))
+            ain_tiles[i] = a_in
+
+        def alpha_quant(i):
+            a_in = ain_tiles[i]
+            s = i % A_SLOTS
+            nc.vector.quantize_mx(
+                out=a_cod[s][:, 64:192].bitcast(FP8X4),
+                scales=a_pl[s][:, 64:192],
+                in_=a_in[:].rearrange("p q j -> p (q j)"),
+            )
+
+        def passes(i):
+            h = i // 2
+            s = i % A_SLOTS
+            acc = ps_o.tile([P, B * F], F32, name="acc")
+            for nl in range(2):
+                xc, xp = xq_tiles[2 * h + nl]
+                nc.tensor.matmul_mx(
+                    out=acc[:],
+                    lhsT=a_cod[s][:, 128 - 128 * nl : 256 - 128 * nl].bitcast(FP8X4),
+                    lhsT_scale=a_pl[s][:, 128 - 128 * nl : 256 - 128 * nl],
+                    rhs=xc[:].bitcast(FP8X4),
+                    rhs_scale=xp[:],
+                    start=(nl == 0),
+                    stop=(nl == 1),
+                )
+            acc_tiles[i] = acc
+
+        def store(h, bh):
+            bs = slice(4 * bh, 4 * bh + 4)
+            nc.sync.dma_start(
+                out=ov[h][:, bs, :], in_=osb_tiles[h][:, bs, :, :].rearrange("q b e f -> q b (e f)")
+            )
+
+        def result_out(i):
+            h, ml = divmod(i, 2)
+            if ml == 0:
+                osb = opool.tile([P, B, 2, F], F32, name="osb")
+                osb_tiles[h] = osb
+            nc.scalar.activation(
+                out=osb_tiles[h][:, :, ml, :],
+                in_=acc_tiles[i][:].rearrange("q (b f) -> q b f", b=B),
+                func=ACT.Copy,
+                scale=rec_tiles[i // 4][:, i % 4 : i % 4 + 1],
+            )
+            if ml == 1:
+                store(h, 0)
+                store(h, 1)
+
+        def last_pair():
+            h = PAIRS - 1
+            osb = opool.tile([P, B, 2, F], F32, name="osb")
+            osb_tiles[h] = osb
+            rec = rec_tiles[(TILES - 1) // 4]
+            accs = {}
+            for nl in range(2):
+                xc, xp = xq_tiles[2 * h + nl]
+                for bh in range(2):
+                    for ml in range(2):
+                        s = (2 * h + ml) % A_SLOTS
+                        if nl == 0:
+                            acc = ps_o.tile([P, 4 * F], F32, name="acc")
+                            accs[(ml, bh)] = acc
+                        nc.tensor.matmul_mx(
+                            out=accs[(ml, bh)][:],
+                            lhsT=a_cod[s][:, 128 - 128 * nl : 256 - 128 * nl].bitcast(FP8X4),
+                            lhsT_scale=a_pl[s][:, 128 - 128 * nl : 256 - 128 * nl],
+                            rhs=xc[:, 256 * bh : 256 * bh + 256].bitcast(FP8X4),
+                            rhs_scale=xp[:, 256 * bh : 256 * bh + 256],
+                            start=(nl == 0),
+                            stop=(nl == 1),
+                        )
+            for bh in range(2):
+                bs = slice(4 * bh, 4 * bh + 4)
+                nc.scalar.activation(
+                    out=osb[:, bs, 0, :], in_=accs[(0, bh)][:].rearrange("q (b f) -> q b f", b=4),
+                    func=ACT.Copy, scale=rec[:, 2:3],
+                )
+                nc.vector.tensor_scalar_mul(
+                    out=osb[:, bs, 1, :], in0=accs[(1, bh)][:].rearrange("q (b f) -> q b f", b=4),
+                    scalar1=rec[:, 3:4],
+                )
+                store(h, bh)
+
+        next_x = 3
+        next_load = PRELOAD
+        pending = [2]
+        for s in range(TILES + 4):
+            if s < TILES:
+                sigmoids(s)
+            if 0 <= s - 1 < TILES:
+                product(s - 1)
+                transposes(s - 1)
+            fresh = []
+            if s not in X_SKIP and next_x < N:
+                if next_x != S_TILE:
+                    x_regroup(next_x, next_x == N - 1)
+                fresh.append(next_x)
+                next_x += 1
+            if 0 <= s - 1 < TILES and (s - 1) % 4 == 3:
+                add_eps((s - 1) // 4)
+            if 0 <= s - 3 < TILES:
+                alpha_quant(s - 3)
+            for n in pending:
+                x_quant(n, n == N - 1)
+            pending = fresh
+            if 0 <= s - 1 < TILES and (s - 1) % 4 == 3:
+                reciprocal((s - 1) // 4)
+            if 0 <= s - 2 < TILES:
+                alpha_out(s - 2)
+            if 0 <= s - 4 < TILES - 2:
+                passes(s - 4)
+            if 0 <= s - 5 < TILES - 2:
+                result_out(s - 5)
+            if s == S_TILE_STEP:
+                x_regroup_scalar(S_TILE)
+            if next_load < N:
+                load_x(next_load)
+                next_load += 1
+        last_pair()

@@ -27,8 +27,7 @@ A_SLOTS = 8
 TILES = 32
 PRELOAD = 12
 X_SKIP = (6, 12, 18, 24, 30)
-S_TILE = 6
-S_TILE_STEP = 2
+S_FROM = 6
 BIASES = (2.0, 1.0, 1.0 / 5.0, 1.0 / 9.0, 1.0 / 13.0)
 SLOPES = (1.0 / 3.0, 1.0 / 7.0, 1.0 / 11.0, 1.0 / 15.0)
 
@@ -55,7 +54,7 @@ def tile_weightedaggregation_kernel(tc, x_aug, t, t_left, t_right, kappa, out):
         xg_tiles = {}
         xq_tiles = {}
         sig_tiles = {}
-        a32_tiles = {}
+        a16_tiles = {}
         den_tiles = {}
         rec_tiles = {}
         at_tiles = {}
@@ -74,20 +73,22 @@ def tile_weightedaggregation_kernel(tc, x_aug, t, t_left, t_right, kappa, out):
             xg = xgrp.tile([P, 4 * B * F], BF16, name="xg", align_bytes=64)
             dst = xg[:].rearrange("p (b c i j) -> p b c j i", b=B, c=16, i=4, j=4)
             src = xr[:].rearrange("p b (j c i) -> p b c j i", j=4, c=16, i=4)
+            xg_tiles[n] = xg
             if halves:
                 nc.vector.tensor_copy(out=dst[:, 0:4], in_=src[:, 0:4])
                 nc.vector.tensor_copy(out=dst[:, 4:8], in_=src[:, 4:8])
+            elif shared(n):
+                nc.vector.tensor_copy(out=dst[:, 0:S_FROM], in_=src[:, 0:S_FROM])
             else:
                 nc.vector.tensor_copy(out=dst, in_=src)
-            xg_tiles[n] = xg
 
-        def x_regroup_scalar(n):
-            xg = xgrp.tile([P, 4 * B * F], BF16, name="xg", align_bytes=64)
-            nc.scalar.copy(
-                out=xg[:].rearrange("p (b f j) -> p b f j", b=B, f=F, j=4),
-                in_=x_tiles[n][:].rearrange("p b (j f) -> p b f j", j=4),
-            )
-            xg_tiles[n] = xg
+        def shared(n):
+            return n == 2 or (n % 2 == 1 and 3 <= n < N - 1)
+
+        def x_regroup_rest(n):
+            dst = xg_tiles[n][:].rearrange("p (b c i j) -> p b c j i", b=B, c=16, i=4, j=4)
+            src = x_tiles[n][:].rearrange("p b (j c i) -> p b c j i", j=4, c=16, i=4)
+            nc.scalar.copy(out=dst[:, S_FROM:B], in_=src[:, S_FROM:B])
 
         def x_quant(n, halves):
             xg = xg_tiles[n]
@@ -167,9 +168,9 @@ def tile_weightedaggregation_kernel(tc, x_aug, t, t_left, t_right, kappa, out):
         k_rd = const.tile([P, 2], F32, name="k_rd")
         nc.vector.reciprocal(out=k_rd[:], in_=k_d[:])
         nc.vector.tensor_copy(out=dst0[:, 4:8], in_=src0[:, 4:8])
-        t_perm = const.tile([P, 4, P], F32, name="t_perm")
-        nc.vector.tensor_copy(out=t_perm[:], in_=t_ps[:].rearrange("q (p j) -> q j p", j=4))
-        t_flat = t_perm[:].rearrange("q j p -> q (j p)")
+        t_perm = const.tile([P, 2, P, 2], F32, name="t_perm")
+        nc.vector.tensor_copy(out=t_perm[:], in_=t_ps[:].rearrange("q (p u e) -> q u p e", u=2, e=2))
+        t_flat = t_perm[:].rearrange("q u p e -> q (u p e)")
 
         k_z = const.tile([P, 2], F32, name="k_z")
         for c in range(2):
@@ -206,6 +207,10 @@ def tile_weightedaggregation_kernel(tc, x_aug, t, t_left, t_right, kappa, out):
         for nl in range(2):
             nc.scalar.activation(out=scaled[:, :, nl, :], in_=raw[:, :, nl, :], func=ACT.Copy,
                                  scale=rk[:, nl : nl + 1])
+        x_regroup(1, False)
+        x_regroup(2, False)
+        x_regroup_rest(2)
+        x_quant(1, False)
         sc_v = scaled[:].rearrange("r g l m -> r g (l m)").rearrange("r g (c e) -> r g e c", e=2)
         tp_ps = ps_a.tile([P, 3, P], F32, name="tp_ps", tag="at")
         tn_ps = ps_a.tile([P, 3, P], F32, name="tn_ps", tag="at")
@@ -220,9 +225,6 @@ def tile_weightedaggregation_kernel(tc, x_aug, t, t_left, t_right, kappa, out):
         tabn = const.tile([P, 3, 16], F32, name="tabn")
         nc.scalar.activation(out=tabn[:], in_=tn_ps[:, :, 0:16], func=ACT.Copy, scale=-1.0)
 
-        x_regroup(1, False)
-        x_regroup(2, False)
-        x_quant(1, False)
 
         def sigmoids(i):
             h, ml = divmod(i, 2)
@@ -240,12 +242,12 @@ def tile_weightedaggregation_kernel(tc, x_aug, t, t_left, t_right, kappa, out):
                 den = small.tile([P, 4], F32, name="den")
                 den_tiles[g] = den
             s1, s2 = sig_tiles[i]
-            a32 = apool.tile([P, L], F32, name="a32")
+            a16 = apool.tile([P, L], BF16, name="a16")
             nc.vector.scalar_tensor_tensor(
-                out=a32[:], in0=s1[:], scalar=1.0, in1=s2[:],
+                out=a16[:], in0=s1[:], scalar=1.0, in1=s2[:],
                 op0=ALU.mult, op1=ALU.mult, accum_out=den_tiles[g][:, c : c + 1],
             )
-            a32_tiles[i] = a32
+            a16_tiles[i] = a16
 
         dene_tiles = {}
 
@@ -260,15 +262,18 @@ def tile_weightedaggregation_kernel(tc, x_aug, t, t_left, t_right, kappa, out):
             rec_tiles[g] = rec
 
         def transposes(i):
-            a32 = a32_tiles[i]
-            at = ps_a.tile([P, 4, P], F32, name="at", tag="at")
-            for j in range(4):
-                nc.tensor.transpose(at[:, j, :], a32[:, j * P : (j + 1) * P], swp[:])
+            words = a16_tiles[i][:].bitcast(F32)
+            at = ps_a.tile([P, 2, P], F32, name="at", tag="at")
+            for u in range(2):
+                nc.tensor.transpose(at[:, u, :], words[:, u * P : (u + 1) * P], swp[:])
             at_tiles[i] = at
 
         def alpha_out(i):
             a_in = apool.tile([P, P, 4], BF16, name="a_in", align_bytes=64)
-            nc.scalar.copy(out=a_in[:], in_=at_tiles[i][:].rearrange("p j q -> p q j"))
+            nc.scalar.copy(
+                out=a_in[:].rearrange("p q j -> p (q j)").bitcast(F32),
+                in_=at_tiles[i][:].rearrange("p u q -> p q u"),
+            )
             ain_tiles[i] = a_in
 
         def alpha_quant(i):
@@ -364,8 +369,7 @@ def tile_weightedaggregation_kernel(tc, x_aug, t, t_left, t_right, kappa, out):
                 transposes(s - 1)
             fresh = []
             if s not in X_SKIP and next_x < N:
-                if next_x != S_TILE:
-                    x_regroup(next_x, next_x == N - 1)
+                x_regroup(next_x, next_x == N - 1)
                 fresh.append(next_x)
                 next_x += 1
             if 0 <= s - 1 < TILES and (s - 1) % 4 == 3:
@@ -383,8 +387,9 @@ def tile_weightedaggregation_kernel(tc, x_aug, t, t_left, t_right, kappa, out):
                 passes(s - 4)
             if 0 <= s - 5 < TILES - 2:
                 result_out(s - 5)
-            if s == S_TILE_STEP:
-                x_regroup_scalar(S_TILE)
+            for n in fresh:
+                if shared(n):
+                    x_regroup_rest(n)
             if next_load < N:
                 load_x(next_load)
                 next_load += 1

@@ -26,8 +26,9 @@ XRAW_BUFS = 24
 A_SLOTS = 8
 TILES = 32
 PRELOAD = 12
-X_SKIP = (6, 12, 18, 24, 30)
+X_SKIP = (5, 10, 15, 20, 25, 30)
 S_FROM = 6
+SIG_PAIRS = 4
 BIASES = (2.0, 1.0, 1.0 / 5.0, 1.0 / 9.0, 1.0 / 13.0)
 SLOPES = (1.0 / 3.0, 1.0 / 7.0, 1.0 / 11.0, 1.0 / 15.0)
 
@@ -42,7 +43,6 @@ def tile_weightedaggregation_kernel(tc, x_aug, t, t_left, t_right, kappa, out):
         xraw = ctx.enter_context(tc.tile_pool(name="xraw", bufs=XRAW_BUFS))
         xgrp = ctx.enter_context(tc.tile_pool(name="xgrp", bufs=4))
         xq = ctx.enter_context(tc.tile_pool(name="xq", bufs=10))
-        sig = ctx.enter_context(tc.tile_pool(name="sig", bufs=4))
         apool = ctx.enter_context(tc.tile_pool(name="apool", bufs=4))
         small = ctx.enter_context(tc.tile_pool(name="small", bufs=4))
         opool = ctx.enter_context(tc.tile_pool(name="opool", bufs=5))
@@ -53,7 +53,6 @@ def tile_weightedaggregation_kernel(tc, x_aug, t, t_left, t_right, kappa, out):
         x_tiles = {}
         xg_tiles = {}
         xq_tiles = {}
-        sig_tiles = {}
         a16_tiles = {}
         den_tiles = {}
         rec_tiles = {}
@@ -76,14 +75,14 @@ def tile_weightedaggregation_kernel(tc, x_aug, t, t_left, t_right, kappa, out):
             xg_tiles[n] = xg
             if halves:
                 nc.vector.tensor_copy(out=dst[:, 0:4], in_=src[:, 0:4])
-                nc.vector.tensor_copy(out=dst[:, 4:8], in_=src[:, 4:8])
+                nc.scalar.copy(out=dst[:, 4:8], in_=src[:, 4:8])
             elif shared(n):
                 nc.vector.tensor_copy(out=dst[:, 0:S_FROM], in_=src[:, 0:S_FROM])
             else:
                 nc.vector.tensor_copy(out=dst, in_=src)
 
         def shared(n):
-            return n == 2 or (n % 2 == 1 and 3 <= n < N - 1)
+            return n in (2, N - 2) or (n % 2 == 1 and 5 <= n < N - 1)
 
         def x_regroup_rest(n):
             dst = xg_tiles[n][:].rearrange("p (b c i j) -> p b c j i", b=B, c=16, i=4, j=4)
@@ -105,28 +104,36 @@ def tile_weightedaggregation_kernel(tc, x_aug, t, t_left, t_right, kappa, out):
                 nc.vector.quantize_mx(out=xc[:].bitcast(FP8X4), scales=xp[:], in_=xg[:])
             xq_tiles[n] = (xc, xp)
 
-        kap = const.tile([P, 2], BF16, name="kap")
-        nc.vector.memset(kap[:], 0.0)
-        nc.scalar.dma_start(out=kap[0:16, :], in_=kappa.rearrange("(h l) o -> h (l o)", l=2))
+        kap = const.tile([PAIRS, 2], BF16, name="kap")
+        nc.sync.dma_start(out=kap[:], in_=kappa.rearrange("(h l) o -> h (l o)", l=2))
         t_row = const.tile([P, L], BF16, name="t_row")
         nc.vector.memset(t_row[:], 0.0)
-        nc.scalar.dma_start(out=t_row[0:1, :], in_=t.rearrange("l o -> o l"))
-        raw = const.tile([P, 3, 2, M], BF16, name="raw")
-        nc.vector.memset(raw[:, 0:2, :, :], 0.0)
-        nc.vector.memset(raw[:, 2, :, :], 1.0)
-        nc.scalar.dma_start(out=raw[0:16, 0, :, :], in_=t_right.rearrange("(h l) m -> h l m", l=2))
-        nc.scalar.dma_start(out=raw[0:16, 1, :, :], in_=t_left.rearrange("(h l) m -> h l m", l=2))
-        for n in range(PRELOAD):
-            load_x(n)
-
         cb = const.tile([P, len(BIASES)], F32, name="cb")
         for i in range(len(BIASES)):
             nc.vector.memset(cb[:, i : i + 1], BIASES[i])
+        s_pairs = []
+        for k in range(SIG_PAIRS):
+            s1 = const.tile([P, L + 2], F32, name="s1_%d" % k)
+            s2 = const.tile([P, L + 2], F32, name="s2_%d" % k)
+            nc.vector.tensor_scalar_mul(out=s1[:, L : L + 1], in0=cb[:, 1:2], scalar1=EPS)
+            nc.vector.memset(s2[:, L : L + 1], 1.0)
+            s_pairs.append((s1, s2))
         warm = const.tile([P, 1], F32, name="warm")
         nc.scalar.activation(out=warm[:], in_=cb[:, 0:1], func=ACT.Sigmoid)
 
+        raw = const.tile([PAIRS, 3, 2, M], BF16, name="raw")
+        nc.vector.memset(raw[:, 2, :, :], 1.0)
+        load_x(0)
+        nc.sync.dma_start(out=t_row[0:1, :], in_=t.rearrange("l o -> o l"))
+        nc.sync.dma_start(out=raw[:, 0, :, :], in_=t_right.rearrange("(h l) m -> h l m", l=2))
+        nc.sync.dma_start(out=raw[:, 1, :, :], in_=t_left.rearrange("(h l) m -> h l m", l=2))
+        for n in range(1, PRELOAD):
+            load_x(n)
+
         ident = const.tile([P, P], F32, name="ident")
         make_identity(nc, ident[:])
+        scaled = const.tile([P, 3, 2, M], F32, name="scaled")
+        nc.gpsimd.memset(scaled[:], 0.0)
         ones_bf = const.tile([P, P], BF16, name="ones_bf")
         nc.vector.memset(ones_bf[:], 1.0)
         a_cod = []
@@ -134,8 +141,8 @@ def tile_weightedaggregation_kernel(tc, x_aug, t, t_left, t_right, kappa, out):
         for s in range(A_SLOTS):
             ac = const.tile([P, 4, 64], U32, name="a_cod%d" % s, align_bytes=64)
             ap = const.tile([P, 4, 64], U8, name="a_pl%d" % s, align_bytes=64)
-            nc.vector.memset(ac[:, 0:4:3, :].bitcast(I32), 0)
-            nc.vector.memset(ap[:, 0:4:3, :].bitcast(I32), 0)
+            nc.gpsimd.memset(ac[:, 0:4:3, :].bitcast(I32), 0)
+            nc.gpsimd.memset(ap[:, 0:4:3, :].bitcast(I32), 0)
             a_cod.append(ac[:].rearrange("p g c -> p (g c)"))
             a_pl.append(ap[:].rearrange("p g c -> p (g c)"))
         swp = const.tile([P, P], F32, name="swp")
@@ -151,13 +158,16 @@ def tile_weightedaggregation_kernel(tc, x_aug, t, t_left, t_right, kappa, out):
         def col(tl, c):
             return tl[:, c : c + 1]
 
-        k_u = const.tile([P, 2], F32, name="k_u")
+        def bias_col(c):
+            return cb[0:PAIRS, c : c + 1]
+
+        k_u = const.tile([PAIRS, 2], F32, name="k_u")
         nc.scalar.activation(out=k_u[:], in_=kap[:], func=ACT.Abs)
-        k_s = const.tile([P, 2], F32, name="k_s")
+        k_s = const.tile([PAIRS, 2], F32, name="k_s")
         nc.scalar.activation(out=k_s[:], in_=k_u[:], func=ACT.Sigmoid, scale=-1.0)
-        k_d = const.tile([P, 2], F32, name="k_d")
-        fma(k_d[:], k_s[:], -1.0, col(cb, 0))
-        k_rl = const.tile([P, 2], F32, name="k_rl")
+        k_d = const.tile([PAIRS, 2], F32, name="k_d")
+        fma(k_d[:], k_s[:], -1.0, bias_col(0))
+        k_rl = const.tile([PAIRS, 2], F32, name="k_rl")
         nc.scalar.activation(out=k_rl[:], in_=kap[:], func=ACT.Relu)
 
         xg0 = xgrp.tile([P, 4 * B * F], BF16, name="xg", align_bytes=64)
@@ -165,52 +175,58 @@ def tile_weightedaggregation_kernel(tc, x_aug, t, t_left, t_right, kappa, out):
         dst0 = xg0[:].rearrange("p (b c i j) -> p b c j i", b=B, c=16, i=4, j=4)
         src0 = x_tiles[0][:].rearrange("p b (j c i) -> p b c j i", j=4, c=16, i=4)
         nc.vector.tensor_copy(out=dst0[:, 0:4], in_=src0[:, 0:4])
-        k_rd = const.tile([P, 2], F32, name="k_rd")
+        k_rd = const.tile([PAIRS, 2], F32, name="k_rd")
         nc.vector.reciprocal(out=k_rd[:], in_=k_d[:])
         nc.vector.tensor_copy(out=dst0[:, 4:8], in_=src0[:, 4:8])
+        x_quant(0, False)
         t_perm = const.tile([P, 2, P, 2], F32, name="t_perm")
-        nc.vector.tensor_copy(out=t_perm[:], in_=t_ps[:].rearrange("q (p u e) -> q u p e", u=2, e=2))
         t_flat = t_perm[:].rearrange("q u p e -> q (u p e)")
 
-        k_z = const.tile([P, 2], F32, name="k_z")
+        k_z = const.tile([PAIRS, 2], F32, name="k_z")
         for c in range(2):
             nc.scalar.activation(out=col(k_z, c), in_=col(k_s, c), func=ACT.Copy, scale=col(k_rd, c))
-        k_z2 = const.tile([P, 2], F32, name="k_z2")
+        k_z2 = const.tile([PAIRS, 2], F32, name="k_z2")
         nc.scalar.activation(out=k_z2[:], in_=k_z[:], func=ACT.Square)
-        k_z4 = const.tile([P, 2], F32, name="k_z4")
+        k_z4 = const.tile([PAIRS, 2], F32, name="k_z4")
         nc.scalar.activation(out=k_z4[:], in_=k_z2[:], func=ACT.Square)
-        k_e = const.tile([P, 4, 2], F32, name="k_e")
+        k_e = const.tile([PAIRS, 4, 2], F32, name="k_e")
         for i in range(4):
-            fma(k_e[:, i, :], k_z2[:], SLOPES[i], col(cb, i + 1))
-        k_z8 = const.tile([P, 2], F32, name="k_z8")
+            fma(k_e[:, i, :], k_z2[:], SLOPES[i], bias_col(i + 1))
+        k_z8 = const.tile([PAIRS, 2], F32, name="k_z8")
         nc.scalar.activation(out=k_z8[:], in_=k_z4[:], func=ACT.Square)
-        k_f = const.tile([P, 2, 2], F32, name="k_f")
+        k_f = const.tile([PAIRS, 2, 2], F32, name="k_f")
         for i in range(2):
             for c in range(2):
                 fma(k_f[:, i, c : c + 1], k_e[:, 2 * i + 1, c : c + 1], col(k_z4, c), k_e[:, 2 * i, c : c + 1])
-        k_g = const.tile([P, 2], F32, name="k_g")
+        k_g = const.tile([PAIRS, 2], F32, name="k_g")
         for c in range(2):
             fma(col(k_g, c), k_f[:, 1, c : c + 1], col(k_z8, c), k_f[:, 0, c : c + 1])
-        k_w = const.tile([P, 2], F32, name="k_w")
+        k_w = const.tile([PAIRS, 2], F32, name="k_w")
         for c in range(2):
             nc.scalar.activation(out=col(k_w, c), in_=col(k_g, c), func=ACT.Copy, scale=col(k_z, c))
 
-        x_quant(0, False)
+        xg1 = xgrp.tile([P, 4 * B * F], BF16, name="xg", align_bytes=64)
+        xg_tiles[1] = xg1
+        dst1 = xg1[:].rearrange("p (b c i j) -> p b c j i", b=B, c=16, i=4, j=4)
+        src1 = x_tiles[1][:].rearrange("p b (j c i) -> p b c j i", j=4, c=16, i=4)
+        nc.vector.tensor_copy(out=dst1[:, 0:4], in_=src1[:, 0:4])
 
-        k_sp = const.tile([P, 2], F32, name="k_sp")
+        k_sp = const.tile([PAIRS, 2], F32, name="k_sp")
         nc.vector.scalar_tensor_tensor(
             out=k_sp[:], in0=k_w[:], scalar=2.0, in1=k_rl[:], op0=ALU.mult, op1=ALU.add
         )
-        rk = const.tile([P, 2], F32, name="rk")
+        rk = const.tile([PAIRS, 2], F32, name="rk")
         nc.vector.reciprocal(out=rk[:], in_=k_sp[:])
-        scaled = const.tile([P, 3, 2, M], F32, name="scaled")
         for nl in range(2):
-            nc.scalar.activation(out=scaled[:, :, nl, :], in_=raw[:, :, nl, :], func=ACT.Copy,
+            nc.scalar.activation(out=scaled[0:PAIRS, :, nl, :], in_=raw[:, :, nl, :], func=ACT.Copy,
                                  scale=rk[:, nl : nl + 1])
-        x_regroup(1, False)
+        nc.vector.tensor_copy(out=dst1[:, 4:8], in_=src1[:, 4:8])
+        nc.vector.tensor_copy(out=t_perm[:], in_=t_ps[:].rearrange("q (p u e) -> q u p e", u=2, e=2))
         x_regroup(2, False)
         x_regroup_rest(2)
         x_quant(1, False)
+        x_regroup(3, False)
+        x_quant(2, False)
         sc_v = scaled[:].rearrange("r g l m -> r g (l m)").rearrange("r g (c e) -> r g e c", e=2)
         tp_ps = ps_a.tile([P, 3, P], F32, name="tp_ps", tag="at")
         tn_ps = ps_a.tile([P, 3, P], F32, name="tn_ps", tag="at")
@@ -228,41 +244,32 @@ def tile_weightedaggregation_kernel(tc, x_aug, t, t_left, t_right, kappa, out):
 
         def sigmoids(i):
             h, ml = divmod(i, 2)
-            s1 = sig.tile([P, L], F32, name="s1")
-            nc.scalar.activation(out=s1[:], in_=t_flat, func=ACT.Sigmoid,
+            s1, s2 = s_pairs[i % SIG_PAIRS]
+            nc.scalar.activation(out=s1[:, 0:L], in_=t_flat, func=ACT.Sigmoid,
                                  scale=tabn[:, 2, h : h + 1], bias=tabp[:, ml, h : h + 1])
-            s2 = sig.tile([P, L], F32, name="s2")
-            nc.scalar.activation(out=s2[:], in_=t_flat, func=ACT.Sigmoid,
+            nc.scalar.activation(out=s2[:, 0:L], in_=t_flat, func=ACT.Sigmoid,
                                  scale=tabp[:, 2, h : h + 1], bias=tabn[:, ml, h : h + 1])
-            sig_tiles[i] = (s1, s2)
 
         def product(i):
             g, c = divmod(i, 4)
             if c == 0:
                 den = small.tile([P, 4], F32, name="den")
                 den_tiles[g] = den
-            s1, s2 = sig_tiles[i]
-            a16 = apool.tile([P, L], BF16, name="a16")
+            s1, s2 = s_pairs[i % SIG_PAIRS]
+            a16 = apool.tile([P, L + 2], BF16, name="a16", align_bytes=64)
             nc.vector.scalar_tensor_tensor(
-                out=a16[:], in0=s1[:], scalar=1.0, in1=s2[:],
+                out=a16[:, 0 : L + 1], in0=s1[:, 0 : L + 1], scalar=1.0, in1=s2[:, 0 : L + 1],
                 op0=ALU.mult, op1=ALU.mult, accum_out=den_tiles[g][:, c : c + 1],
             )
             a16_tiles[i] = a16
 
-        dene_tiles = {}
-
-        def add_eps(g):
-            dene = small.tile([P, 4], F32, name="dene")
-            nc.vector.tensor_scalar_add(out=dene[:], in0=den_tiles[g][:], scalar1=EPS)
-            dene_tiles[g] = dene
-
         def reciprocal(g):
             rec = small.tile([P, 4], F32, name="rec")
-            nc.vector.reciprocal(out=rec[:], in_=dene_tiles[g][:])
+            nc.vector.reciprocal(out=rec[:], in_=den_tiles[g][:])
             rec_tiles[g] = rec
 
         def transposes(i):
-            words = a16_tiles[i][:].bitcast(F32)
+            words = a16_tiles[i][:, 0:L].bitcast(F32)
             at = ps_a.tile([P, 2, P], F32, name="at", tag="at")
             for u in range(2):
                 nc.tensor.transpose(at[:, u, :], words[:, u * P : (u + 1) * P], swp[:])
@@ -358,9 +365,9 @@ def tile_weightedaggregation_kernel(tc, x_aug, t, t_left, t_right, kappa, out):
                 )
                 store(h, bh)
 
-        next_x = 3
+        next_x = 4
         next_load = PRELOAD
-        pending = [2]
+        pending = [3]
         for s in range(TILES + 4):
             if s < TILES:
                 sigmoids(s)
@@ -372,24 +379,22 @@ def tile_weightedaggregation_kernel(tc, x_aug, t, t_left, t_right, kappa, out):
                 x_regroup(next_x, next_x == N - 1)
                 fresh.append(next_x)
                 next_x += 1
-            if 0 <= s - 1 < TILES and (s - 1) % 4 == 3:
-                add_eps((s - 1) // 4)
             if 0 <= s - 3 < TILES:
                 alpha_quant(s - 3)
+            if 0 <= s - 1 < TILES and (s - 1) % 4 == 3:
+                reciprocal((s - 1) // 4)
             for n in pending:
                 x_quant(n, n == N - 1)
             pending = fresh
-            if 0 <= s - 1 < TILES and (s - 1) % 4 == 3:
-                reciprocal((s - 1) // 4)
+            for n in fresh:
+                if shared(n):
+                    x_regroup_rest(n)
             if 0 <= s - 2 < TILES:
                 alpha_out(s - 2)
             if 0 <= s - 4 < TILES - 2:
                 passes(s - 4)
             if 0 <= s - 5 < TILES - 2:
                 result_out(s - 5)
-            for n in fresh:
-                if shared(n):
-                    x_regroup_rest(n)
             if next_load < N:
                 load_x(next_load)
                 next_load += 1

@@ -26,7 +26,7 @@ XRAW_BUFS = 24
 A_SLOTS = 8
 TILES = 32
 PRELOAD = 12
-X_SKIP = (5, 10, 15, 20, 25, 30)
+X_SKIP = (6, 12, 18, 24, 30)
 S_FROM = 6
 SIG_PAIRS = 4
 BIASES = (2.0, 1.0, 1.0 / 5.0, 1.0 / 9.0, 1.0 / 13.0)
@@ -46,8 +46,9 @@ def tile_weightedaggregation_kernel(tc, x_aug, t, t_left, t_right, kappa, out):
         apool = ctx.enter_context(tc.tile_pool(name="apool", bufs=4))
         small = ctx.enter_context(tc.tile_pool(name="small", bufs=4))
         opool = ctx.enter_context(tc.tile_pool(name="opool", bufs=5))
-        ps_a = ctx.enter_context(tc.psum_pool(name="ps_a", bufs=4))
+        ps_a = ctx.enter_context(tc.psum_pool(name="ps_a", bufs=3))
         ps_o = ctx.enter_context(tc.psum_pool(name="ps_o", bufs=4))
+        ps_x = ctx.enter_context(tc.psum_pool(name="ps_x", bufs=1))
         ctx.enter_context(tc.manual_schedule())
 
         x_tiles = {}
@@ -63,8 +64,8 @@ def tile_weightedaggregation_kernel(tc, x_aug, t, t_left, t_right, kappa, out):
 
         def load_x(n):
             xr = xraw.tile([P, B, 4 * F], BF16, name="xr")
-            nc.sync.dma_start(out=xr[:, 0:4, :], in_=xv[n][:, 0:4, :])
-            nc.sync.dma_start(out=xr[:, 4:8, :], in_=xv[n][:, 4:8, :])
+            for a, z in ((0, 2), (2, 4), (4, 8)) if n == 0 else ((0, 4), (4, 8)):
+                nc.sync.dma_start(out=xr[:, a:z, :], in_=xv[n][:, a:z, :])
             x_tiles[n] = xr
 
         def x_regroup(n, halves):
@@ -82,9 +83,27 @@ def tile_weightedaggregation_kernel(tc, x_aug, t, t_left, t_right, kappa, out):
                 nc.vector.tensor_copy(out=dst, in_=src)
 
         def shared(n):
-            return n in (2, N - 2) or (n % 2 == 1 and 5 <= n < N - 1)
+            return n in (2, N - 2) or (n % 2 == 1 and 3 <= n < N - 1)
+
+        def spread(n):
+            return shared(n) and 9 <= n < N - 2
+
+        spread_tiles = {}
+
+        def x_spread(n):
+            xs = ps_x.tile([P, (B - S_FROM) * 4 * F], BF16, name="xs")
+            nc.tensor.matmul(
+                xs[:].rearrange("p (b f j) -> p b j f", b=B - S_FROM, j=4),
+                lhsT=ident_bf[:],
+                rhs=x_tiles[n][:, S_FROM:B, :].rearrange("p b (j f) -> p b j f", j=4),
+                start=True, stop=True,
+            )
+            spread_tiles[n] = xs
 
         def x_regroup_rest(n):
+            if spread(n):
+                nc.scalar.copy(out=xg_tiles[n][:, S_FROM * 4 * F : B * 4 * F], in_=spread_tiles[n][:])
+                return
             dst = xg_tiles[n][:].rearrange("p (b c i j) -> p b c j i", b=B, c=16, i=4, j=4)
             src = x_tiles[n][:].rearrange("p b (j c i) -> p b c j i", j=4, c=16, i=4)
             nc.scalar.copy(out=dst[:, S_FROM:B], in_=src[:, S_FROM:B])
@@ -94,11 +113,11 @@ def tile_weightedaggregation_kernel(tc, x_aug, t, t_left, t_right, kappa, out):
             xc = xq.tile([P, B * F], U32, name="xc", align_bytes=64)
             xp = xq.tile([P, B * F], U8, name="xp", align_bytes=64)
             if halves:
-                for bh in range(2):
+                for k in range(4):
                     nc.vector.quantize_mx(
-                        out=xc[:, 256 * bh : 256 * bh + 256].bitcast(FP8X4),
-                        scales=xp[:, 256 * bh : 256 * bh + 256],
-                        in_=xg[:, 1024 * bh : 1024 * bh + 1024],
+                        out=xc[:, 128 * k : 128 * k + 128].bitcast(FP8X4),
+                        scales=xp[:, 128 * k : 128 * k + 128],
+                        in_=xg[:, 512 * k : 512 * k + 512],
                     )
             else:
                 nc.vector.quantize_mx(out=xc[:].bitcast(FP8X4), scales=xp[:], in_=xg[:])
@@ -134,6 +153,8 @@ def tile_weightedaggregation_kernel(tc, x_aug, t, t_left, t_right, kappa, out):
         make_identity(nc, ident[:])
         scaled = const.tile([P, 3, 2, M], F32, name="scaled")
         nc.gpsimd.memset(scaled[:], 0.0)
+        ident_bf = const.tile([P, P], BF16, name="ident_bf")
+        nc.vector.tensor_copy(out=ident_bf[:], in_=ident[:])
         ones_bf = const.tile([P, P], BF16, name="ones_bf")
         nc.vector.memset(ones_bf[:], 1.0)
         a_cod = []
@@ -174,7 +195,8 @@ def tile_weightedaggregation_kernel(tc, x_aug, t, t_left, t_right, kappa, out):
         xg_tiles[0] = xg0
         dst0 = xg0[:].rearrange("p (b c i j) -> p b c j i", b=B, c=16, i=4, j=4)
         src0 = x_tiles[0][:].rearrange("p b (j c i) -> p b c j i", j=4, c=16, i=4)
-        nc.vector.tensor_copy(out=dst0[:, 0:4], in_=src0[:, 0:4])
+        nc.vector.tensor_copy(out=dst0[:, 0:2], in_=src0[:, 0:2])
+        nc.vector.tensor_copy(out=dst0[:, 2:4], in_=src0[:, 2:4])
         k_rd = const.tile([PAIRS, 2], F32, name="k_rd")
         nc.vector.reciprocal(out=k_rd[:], in_=k_d[:])
         nc.vector.tensor_copy(out=dst0[:, 4:8], in_=src0[:, 4:8])
@@ -210,6 +232,7 @@ def tile_weightedaggregation_kernel(tc, x_aug, t, t_left, t_right, kappa, out):
         dst1 = xg1[:].rearrange("p (b c i j) -> p b c j i", b=B, c=16, i=4, j=4)
         src1 = x_tiles[1][:].rearrange("p b (j c i) -> p b c j i", j=4, c=16, i=4)
         nc.vector.tensor_copy(out=dst1[:, 0:4], in_=src1[:, 0:4])
+        nc.scalar.copy(out=dst1[:, 6:8], in_=src1[:, 6:8])
 
         k_sp = const.tile([PAIRS, 2], F32, name="k_sp")
         nc.vector.scalar_tensor_tensor(
@@ -220,13 +243,11 @@ def tile_weightedaggregation_kernel(tc, x_aug, t, t_left, t_right, kappa, out):
         for nl in range(2):
             nc.scalar.activation(out=scaled[0:PAIRS, :, nl, :], in_=raw[:, :, nl, :], func=ACT.Copy,
                                  scale=rk[:, nl : nl + 1])
-        nc.vector.tensor_copy(out=dst1[:, 4:8], in_=src1[:, 4:8])
+        nc.vector.tensor_copy(out=dst1[:, 4:6], in_=src1[:, 4:6])
         nc.vector.tensor_copy(out=t_perm[:], in_=t_ps[:].rearrange("q (p u e) -> q u p e", u=2, e=2))
         x_regroup(2, False)
         x_regroup_rest(2)
         x_quant(1, False)
-        x_regroup(3, False)
-        x_quant(2, False)
         sc_v = scaled[:].rearrange("r g l m -> r g (l m)").rearrange("r g (c e) -> r g e c", e=2)
         tp_ps = ps_a.tile([P, 3, P], F32, name="tp_ps", tag="at")
         tn_ps = ps_a.tile([P, 3, P], F32, name="tn_ps", tag="at")
@@ -309,8 +330,7 @@ def tile_weightedaggregation_kernel(tc, x_aug, t, t_left, t_right, kappa, out):
                 )
             acc_tiles[i] = acc
 
-        def store(h, bh):
-            bs = slice(4 * bh, 4 * bh + 4)
+        def store(h, bs):
             nc.sync.dma_start(
                 out=ov[h][:, bs, :], in_=osb_tiles[h][:, bs, :, :].rearrange("q b e f -> q b (e f)")
             )
@@ -327,47 +347,46 @@ def tile_weightedaggregation_kernel(tc, x_aug, t, t_left, t_right, kappa, out):
                 scale=rec_tiles[i // 4][:, i % 4 : i % 4 + 1],
             )
             if ml == 1:
-                store(h, 0)
-                store(h, 1)
+                store(h, slice(0, 4))
+                store(h, slice(4, 8))
 
         def last_pair():
             h = PAIRS - 1
             osb = opool.tile([P, B, 2, F], F32, name="osb")
             osb_tiles[h] = osb
             rec = rec_tiles[(TILES - 1) // 4]
-            accs = {}
-            for nl in range(2):
-                xc, xp = xq_tiles[2 * h + nl]
-                for bh in range(2):
-                    for ml in range(2):
-                        s = (2 * h + ml) % A_SLOTS
-                        if nl == 0:
-                            acc = ps_o.tile([P, 4 * F], F32, name="acc")
-                            accs[(ml, bh)] = acc
+            for k in range(4):
+                cols = slice(128 * k, 128 * k + 128)
+                accs = []
+                for ml in range(2):
+                    s = (2 * h + ml) % A_SLOTS
+                    acc = ps_o.tile([P, 2 * F], F32, name="acc")
+                    accs.append(acc)
+                    for nl in range(2):
+                        xc, xp = xq_tiles[2 * h + nl]
                         nc.tensor.matmul_mx(
-                            out=accs[(ml, bh)][:],
+                            out=acc[:],
                             lhsT=a_cod[s][:, 128 - 128 * nl : 256 - 128 * nl].bitcast(FP8X4),
                             lhsT_scale=a_pl[s][:, 128 - 128 * nl : 256 - 128 * nl],
-                            rhs=xc[:, 256 * bh : 256 * bh + 256].bitcast(FP8X4),
-                            rhs_scale=xp[:, 256 * bh : 256 * bh + 256],
+                            rhs=xc[:, cols].bitcast(FP8X4),
+                            rhs_scale=xp[:, cols],
                             start=(nl == 0),
                             stop=(nl == 1),
                         )
-            for bh in range(2):
-                bs = slice(4 * bh, 4 * bh + 4)
+                bs = slice(2 * k, 2 * k + 2)
                 nc.scalar.activation(
-                    out=osb[:, bs, 0, :], in_=accs[(0, bh)][:].rearrange("q (b f) -> q b f", b=4),
+                    out=osb[:, bs, 0, :], in_=accs[0][:].rearrange("q (b f) -> q b f", b=2),
                     func=ACT.Copy, scale=rec[:, 2:3],
                 )
                 nc.vector.tensor_scalar_mul(
-                    out=osb[:, bs, 1, :], in0=accs[(1, bh)][:].rearrange("q (b f) -> q b f", b=4),
+                    out=osb[:, bs, 1, :], in0=accs[1][:].rearrange("q (b f) -> q b f", b=2),
                     scalar1=rec[:, 3:4],
                 )
-                store(h, bh)
+                store(h, bs)
 
-        next_x = 4
+        next_x = 3
         next_load = PRELOAD
-        pending = [3]
+        pending = [2]
         for s in range(TILES + 4):
             if s < TILES:
                 sigmoids(s)
@@ -393,6 +412,8 @@ def tile_weightedaggregation_kernel(tc, x_aug, t, t_left, t_right, kappa, out):
                 alpha_out(s - 2)
             if 0 <= s - 4 < TILES - 2:
                 passes(s - 4)
+            if s + 1 not in X_SKIP and next_x < N and spread(next_x):
+                x_spread(next_x)
             if 0 <= s - 5 < TILES - 2:
                 result_out(s - 5)
             if next_load < N:

@@ -83,10 +83,10 @@ def tile_weightedaggregation_kernel(tc, x_aug, t, t_left, t_right, kappa, out):
                 nc.vector.tensor_copy(out=dst, in_=src)
 
         def shared(n):
-            return n in (2, N - 2) or (n % 2 == 1 and 3 <= n < N - 1)
+            return n in (2, N - 2) or (n % 2 == 1 and 5 <= n < N - 1) or (n % 8 == 4)
 
         def spread(n):
-            return shared(n) and 9 <= n < N - 2
+            return n % 2 == 1 and 9 <= n < N - 2
 
         spread_tiles = {}
 

@@ -141,17 +141,17 @@ def tile_weightedaggregation_kernel(tc, x_aug, t, t_left, t_right, kappa, out):
         nc.scalar.activation(out=warm[:], in_=cb[:, 0:1], func=ACT.Sigmoid)
 
         raw = const.tile([PAIRS, 3, 2, M], BF16, name="raw")
-        nc.vector.memset(raw[:, 2, :, :], 1.0)
+        nc.vector.memset(raw[:, 1, :, :], 1.0)
         load_x(0)
         nc.sync.dma_start(out=t_row[0:1, :], in_=t.rearrange("l o -> o l"))
         nc.sync.dma_start(out=raw[:, 0, :, :], in_=t_right.rearrange("(h l) m -> h l m", l=2))
-        nc.sync.dma_start(out=raw[:, 1, :, :], in_=t_left.rearrange("(h l) m -> h l m", l=2))
+        nc.sync.dma_start(out=raw[:, 2, :, :], in_=t_left.rearrange("(h l) m -> h l m", l=2))
         for n in range(1, PRELOAD):
             load_x(n)
 
         ident = const.tile([P, P], F32, name="ident")
         make_identity(nc, ident[:])
-        scaled = const.tile([P, 3, 2, M], F32, name="scaled")
+        scaled = const.tile([P, 2, 3, P], F32, name="scaled")
         nc.gpsimd.memset(scaled[:], 0.0)
         ident_bf = const.tile([P, P], BF16, name="ident_bf")
         nc.vector.tensor_copy(out=ident_bf[:], in_=ident[:])
@@ -240,36 +240,40 @@ def tile_weightedaggregation_kernel(tc, x_aug, t, t_left, t_right, kappa, out):
         )
         rk = const.tile([PAIRS, 2], F32, name="rk")
         nc.vector.reciprocal(out=rk[:], in_=k_sp[:])
-        for nl in range(2):
-            nc.scalar.activation(out=scaled[0:PAIRS, :, nl, :], in_=raw[:, :, nl, :], func=ACT.Copy,
-                                 scale=rk[:, nl : nl + 1])
+        raw_v = raw[:].rearrange("h g l (c e) -> h e g l c", e=2)
+        scaled_v = scaled[0:PAIRS].rearrange("h e g (l c) -> h e g l c", l=2)
+        for ml in range(2):
+            for nl in range(2):
+                nc.scalar.activation(out=scaled_v[:, ml, :, nl, :], in_=raw_v[:, ml, :, nl, :], func=ACT.Copy,
+                                     scale=rk[:, nl : nl + 1])
         nc.vector.tensor_copy(out=dst1[:, 4:6], in_=src1[:, 4:6])
         nc.vector.tensor_copy(out=t_perm[:], in_=t_ps[:].rearrange("q (p u e) -> q u p e", u=2, e=2))
         x_regroup(2, False)
         x_regroup_rest(2)
         x_quant(1, False)
-        sc_v = scaled[:].rearrange("r g l m -> r g (l m)").rearrange("r g (c e) -> r g e c", e=2)
-        tp_ps = ps_a.tile([P, 3, P], F32, name="tp_ps", tag="at")
-        tn_ps = ps_a.tile([P, 3, P], F32, name="tn_ps", tag="at")
+        tabs = []
         for ml in range(2):
-            nc.tensor.transpose(tp_ps[:, ml, :], sc_v[:, 0, ml, :], ident[:])
-        nc.tensor.transpose(tp_ps[:, 2, :], sc_v[:, 2, 0, :], ident[:])
-        for ml in range(2):
-            nc.tensor.transpose(tn_ps[:, ml, :], sc_v[:, 1, ml, :], ident[:])
-        nc.tensor.transpose(tn_ps[:, 2, :], sc_v[:, 2, 0, :], ident[:])
-        tabp = const.tile([P, 3, 16], F32, name="tabp")
-        nc.scalar.copy(out=tabp[:], in_=tp_ps[:, :, 0:16])
-        tabn = const.tile([P, 3, 16], F32, name="tabn")
-        nc.scalar.activation(out=tabn[:], in_=tn_ps[:, :, 0:16], func=ACT.Copy, scale=-1.0)
+            tab_ps = ps_a.tile([P, 3, P], F32, name="tab_ps", tag="at")
+            for g in range(3):
+                nc.tensor.transpose(tab_ps[:, g, :], scaled[:, ml, g, :], ident[:])
+            tabs.append((tab_ps, const.tile([P, 2, PAIRS], F32, name="tp%d" % ml),
+                         const.tile([P, 2, PAIRS], F32, name="tn%d" % ml)))
 
+        def tables(ml):
+            tab_ps, tp, tn = tabs[ml]
+            nc.scalar.copy(out=tp[:], in_=tab_ps[:, 0:2, 0:PAIRS])
+            nc.scalar.activation(out=tn[:], in_=tab_ps[:, 1:3, 0:PAIRS], func=ACT.Copy, scale=-1.0)
 
         def sigmoids(i):
             h, ml = divmod(i, 2)
+            if h == 0:
+                tables(ml)
+            tab_ps, tp, tn = tabs[ml]
             s1, s2 = s_pairs[i % SIG_PAIRS]
             nc.scalar.activation(out=s1[:, 0:L], in_=t_flat, func=ACT.Sigmoid,
-                                 scale=tabn[:, 2, h : h + 1], bias=tabp[:, ml, h : h + 1])
+                                 scale=tn[:, 0, h : h + 1], bias=tp[:, 0, h : h + 1])
             nc.scalar.activation(out=s2[:, 0:L], in_=t_flat, func=ACT.Sigmoid,
-                                 scale=tabp[:, 2, h : h + 1], bias=tabn[:, ml, h : h + 1])
+                                 scale=tp[:, 1, h : h + 1], bias=tn[:, 1, h : h + 1])
 
         def product(i):
             g, c = divmod(i, 4)
@@ -388,6 +392,9 @@ def tile_weightedaggregation_kernel(tc, x_aug, t, t_left, t_right, kappa, out):
         next_load = PRELOAD
         pending = [2]
         for s in range(TILES + 4):
+            ahead = next_x + 1 if s not in X_SKIP else next_x
+            if s + 1 not in X_SKIP and ahead < N and spread(ahead):
+                x_spread(ahead)
             if s < TILES:
                 sigmoids(s)
             if 0 <= s - 1 < TILES:
@@ -412,8 +419,6 @@ def tile_weightedaggregation_kernel(tc, x_aug, t, t_left, t_right, kappa, out):
                 alpha_out(s - 2)
             if 0 <= s - 4 < TILES - 2:
                 passes(s - 4)
-            if s + 1 not in X_SKIP and next_x < N and spread(next_x):
-                x_spread(next_x)
             if 0 <= s - 5 < TILES - 2:
                 result_out(s - 5)
             if next_load < N:

from contextlib import ExitStack

import concourse.mybir as mybir
from concourse.masks import make_identity

F32 = mybir.dt.float32
BF16 = mybir.dt.bfloat16
U32 = mybir.dt.uint32
I32 = mybir.dt.int32
U8 = mybir.dt.uint8
FP8X4 = mybir.dt.float8_e4m3fn_x4
ACT = mybir.ActivationFunctionType
ALU = mybir.AluOpType

B = 8
N = 32
L = 512
M = 128
F = 64
EPS = 1e-8
P = 128
PAIRS = N // 2
FLOPS = 2 * B * N * M * F * L

XRAW_BUFS = 24
A_SLOTS = 8
TILES = 32
PRELOAD = 12
X_SKIP = (6, 12, 18, 24, 30)
S_FROM = 6
SIG_PAIRS = 4
BIASES = (2.0, 1.0, 1.0 / 5.0, 1.0 / 9.0, 1.0 / 13.0)
SLOPES = (1.0 / 3.0, 1.0 / 7.0, 1.0 / 11.0, 1.0 / 15.0)


def tile_weightedaggregation_kernel(tc, x_aug, t, t_left, t_right, kappa, out):
    nc = tc.nc
    xv = x_aug.rearrange("b n (p j) f -> n p b (j f)", j=4)
    ov = out.rearrange("b (h nl) (mh ml) f -> h (nl mh) b (ml f)", nl=2, ml=2)

    with ExitStack() as ctx:
        const = ctx.enter_context(tc.tile_pool(name="const", bufs=1))
        xraw = ctx.enter_context(tc.tile_pool(name="xraw", bufs=XRAW_BUFS))
        xgrp = ctx.enter_context(tc.tile_pool(name="xgrp", bufs=4))
        xq = ctx.enter_context(tc.tile_pool(name="xq", bufs=10))
        apool = ctx.enter_context(tc.tile_pool(name="apool", bufs=4))
        small = ctx.enter_context(tc.tile_pool(name="small", bufs=4))
        opool = ctx.enter_context(tc.tile_pool(name="opool", bufs=5))
        ps_a = ctx.enter_context(tc.psum_pool(name="ps_a", bufs=3))
        ps_o = ctx.enter_context(tc.psum_pool(name="ps_o", bufs=4))
        ps_x = ctx.enter_context(tc.psum_pool(name="ps_x", bufs=1))
        ctx.enter_context(tc.manual_schedule())

        x_tiles = {}
        xg_tiles = {}
        xq_tiles = {}
        a16_tiles = {}
        den_tiles = {}
        rec_tiles = {}
        at_tiles = {}
        ain_tiles = {}
        acc_tiles = {}
        osb_tiles = {}

        def load_x(n):
            xr = xraw.tile([P, B, 4 * F], BF16, name="xr")
            for a, z in ((0, 2), (2, 4), (4, 8)) if n == 0 else ((0, 4), (4, 8)):
                nc.sync.dma_start(out=xr[:, a:z, :], in_=xv[n][:, a:z, :])
            x_tiles[n] = xr

        def x_regroup(n, halves):
            xr = x_tiles[n]
            xg = xgrp.tile([P, 4 * B * F], BF16, name="xg", align_bytes=64)
            dst = xg[:].rearrange("p (b c i j) -> p b c j i", b=B, c=16, i=4, j=4)
            src = xr[:].rearrange("p b (j c i) -> p b c j i", j=4, c=16, i=4)
            xg_tiles[n] = xg
            if halves:
                nc.vector.tensor_copy(out=dst[:, 0:4], in_=src[:, 0:4])
                nc.scalar.copy(out=dst[:, 4:8], in_=src[:, 4:8])
            elif shared(n):
                nc.vector.tensor_copy(out=dst[:, 0:S_FROM], in_=src[:, 0:S_FROM])
            else:
                nc.vector.tensor_copy(out=dst, in_=src)

        def shared(n):
            return n in (2, N - 2) or (n % 2 == 1 and 5 <= n < N - 1) or (n % 8 == 4)

        def spread(n):
            return n % 2 == 1 and 9 <= n < N - 2

        spread_tiles = {}

        def x_spread(n):
            xs = ps_x.tile([P, (B - S_FROM) * 4 * F], BF16, name="xs")
            nc.tensor.matmul(
                xs[:].rearrange("p (b f j) -> p b j f", b=B - S_FROM, j=4),
                lhsT=ident_bf[:],
                rhs=x_tiles[n][:, S_FROM:B, :].rearrange("p b (j f) -> p b j f", j=4),
                start=True, stop=True,
            )
            spread_tiles[n] = xs

        def x_regroup_rest(n):
            if spread(n):
                nc.scalar.copy(out=xg_tiles[n][:, S_FROM * 4 * F : B * 4 * F], in_=spread_tiles[n][:])
                return
            dst = xg_tiles[n][:].rearrange("p (b c i j) -> p b c j i", b=B, c=16, i=4, j=4)
            src = x_tiles[n][:].rearrange("p b (j c i) -> p b c j i", j=4, c=16, i=4)
            nc.scalar.copy(out=dst[:, S_FROM:B], in_=src[:, S_FROM:B])

        def x_quant(n, halves):
            xg = xg_tiles[n]
            xc = xq.tile([P, B * F], U32, name="xc", align_bytes=64)
            xp = xq.tile([P, B * F], U8, name="xp", align_bytes=64)
            if halves:
                for k in range(4):
                    nc.vector.quantize_mx(
                        out=xc[:, 128 * k : 128 * k + 128].bitcast(FP8X4),
                        scales=xp[:, 128 * k : 128 * k + 128],
                        in_=xg[:, 512 * k : 512 * k + 512],
                    )
            else:
                nc.vector.quantize_mx(out=xc[:].bitcast(FP8X4), scales=xp[:], in_=xg[:])
            xq_tiles[n] = (xc, xp)

        kap = const.tile([PAIRS, 2], BF16, name="kap")
        nc.sync.dma_start(out=kap[:], in_=kappa.rearrange("(h l) o -> h (l o)", l=2))
        t_row = const.tile([P, L], BF16, name="t_row")
        nc.vector.memset(t_row[:], 0.0)
        cb = const.tile([P, len(BIASES)], F32, name="cb")
        for i in range(len(BIASES)):
            nc.vector.memset(cb[:, i : i + 1], BIASES[i])
        s_pairs = []
        for k in range(SIG_PAIRS):
            s1 = const.tile([P, L + 2], F32, name="s1_%d" % k)
            s2 = const.tile([P, L + 2], F32, name="s2_%d" % k)
            nc.vector.tensor_scalar_mul(out=s1[:, L : L + 1], in0=cb[:, 1:2], scalar1=EPS)
            nc.vector.memset(s2[:, L : L + 1], 1.0)
            s_pairs.append((s1, s2))
        warm = const.tile([P, 1], F32, name="warm")
        nc.scalar.activation(out=warm[:], in_=cb[:, 0:1], func=ACT.Sigmoid)

        raw = const.tile([PAIRS, 3, 2, M], BF16, name="raw")
        nc.vector.memset(raw[:, 1, :, :], 1.0)
        load_x(0)
        nc.sync.dma_start(out=t_row[0:1, :], in_=t.rearrange("l o -> o l"))
        nc.sync.dma_start(out=raw[:, 0, :, :], in_=t_right.rearrange("(h l) m -> h l m", l=2))
        nc.sync.dma_start(out=raw[:, 2, :, :], in_=t_left.rearrange("(h l) m -> h l m", l=2))
        for n in range(1, PRELOAD):
            load_x(n)

        ident = const.tile([P, P], F32, name="ident")
        make_identity(nc, ident[:])
        scaled = const.tile([P, 2, 3, P], F32, name="scaled")
        nc.gpsimd.memset(scaled[:], 0.0)
        ident_bf = const.tile([P, P], BF16, name="ident_bf")
        nc.vector.tensor_copy(out=ident_bf[:], in_=ident[:])
        ones_bf = const.tile([P, P], BF16, name="ones_bf")
        nc.vector.memset(ones_bf[:], 1.0)
        a_cod = []
        a_pl = []
        for s in range(A_SLOTS):
            ac = const.tile([P, 4, 64], U32, name="a_cod%d" % s, align_bytes=64)
            ap = const.tile([P, 4, 64], U8, name="a_pl%d" % s, align_bytes=64)
            nc.gpsimd.memset(ac[:, 0:4:3, :].bitcast(I32), 0)
            nc.gpsimd.memset(ap[:, 0:4:3, :].bitcast(I32), 0)
            a_cod.append(ac[:].rearrange("p g c -> p (g c)"))
            a_pl.append(ap[:].rearrange("p g c -> p (g c)"))
        swp = const.tile([P, P], F32, name="swp")
        nc.vector.tensor_copy(out=swp[:, 0:64], in_=ident[:, 64:128])
        nc.vector.tensor_copy(out=swp[:, 64:128], in_=ident[:, 0:64])

        t_ps = ps_a.tile([P, L], F32, name="t_ps", tag="at")
        nc.tensor.matmul(t_ps[:], lhsT=ones_bf[:], rhs=t_row[:], start=True, stop=True)

        def fma(out, in_, scale, bias):
            nc.scalar.activation(out=out, in_=in_, func=ACT.Identity, scale=scale, bias=bias)

        def col(tl, c):
            return tl[:, c : c + 1]

        def bias_col(c):
            return cb[0:PAIRS, c : c + 1]

        k_u = const.tile([PAIRS, 2], F32, name="k_u")
        nc.scalar.activation(out=k_u[:], in_=kap[:], func=ACT.Abs)
        k_s = const.tile([PAIRS, 2], F32, name="k_s")
        nc.scalar.activation(out=k_s[:], in_=k_u[:], func=ACT.Sigmoid, scale=-1.0)
        k_d = const.tile([PAIRS, 2], F32, name="k_d")
        fma(k_d[:], k_s[:], -1.0, bias_col(0))
        k_rl = const.tile([PAIRS, 2], F32, name="k_rl")
        nc.scalar.activation(out=k_rl[:], in_=kap[:], func=ACT.Relu)

        xg0 = xgrp.tile([P, 4 * B * F], BF16, name="xg", align_bytes=64)
        xg_tiles[0] = xg0
        dst0 = xg0[:].rearrange("p (b c i j) -> p b c j i", b=B, c=16, i=4, j=4)
        src0 = x_tiles[0][:].rearrange("p b (j c i) -> p b c j i", j=4, c=16, i=4)
        nc.vector.tensor_copy(out=dst0[:, 0:2], in_=src0[:, 0:2])
        nc.vector.tensor_copy(out=dst0[:, 2:4], in_=src0[:, 2:4])
        k_rd = const.tile([PAIRS, 2], F32, name="k_rd")
        nc.vector.reciprocal(out=k_rd[:], in_=k_d[:])
        nc.vector.tensor_copy(out=dst0[:, 4:8], in_=src0[:, 4:8])
        x_quant(0, False)
        t_perm = const.tile([P, 2, P, 2], F32, name="t_perm")
        t_flat = t_perm[:].rearrange("q u p e -> q (u p e)")

        k_z = const.tile([PAIRS, 2], F32, name="k_z")
        for c in range(2):
            nc.scalar.activation(out=col(k_z, c), in_=col(k_s, c), func=ACT.Copy, scale=col(k_rd, c))
        k_z2 = const.tile([PAIRS, 2], F32, name="k_z2")
        nc.scalar.activation(out=k_z2[:], in_=k_z[:], func=ACT.Square)
        k_z4 = const.tile([PAIRS, 2], F32, name="k_z4")
        nc.scalar.activation(out=k_z4[:], in_=k_z2[:], func=ACT.Square)
        k_e = const.tile([PAIRS, 4, 2], F32, name="k_e")
        for i in range(4):
            fma(k_e[:, i, :], k_z2[:], SLOPES[i], bias_col(i + 1))
        k_z8 = const.tile([PAIRS, 2], F32, name="k_z8")
        nc.scalar.activation(out=k_z8[:], in_=k_z4[:], func=ACT.Square)
        k_f = const.tile([PAIRS, 2, 2], F32, name="k_f")
        for i in range(2):
            for c in range(2):
                fma(k_f[:, i, c : c + 1], k_e[:, 2 * i + 1, c : c + 1], col(k_z4, c), k_e[:, 2 * i, c : c + 1])
        k_g = const.tile([PAIRS, 2], F32, name="k_g")
        for c in range(2):
            fma(col(k_g, c), k_f[:, 1, c : c + 1], col(k_z8, c), k_f[:, 0, c : c + 1])
        k_w = const.tile([PAIRS, 2], F32, name="k_w")
        for c in range(2):
            nc.scalar.activation(out=col(k_w, c), in_=col(k_g, c), func=ACT.Copy, scale=col(k_z, c))

        xg1 = xgrp.tile([P, 4 * B * F], BF16, name="xg", align_bytes=64)
        xg_tiles[1] = xg1
        dst1 = xg1[:].rearrange("p (b c i j) -> p b c j i", b=B, c=16, i=4, j=4)
        src1 = x_tiles[1][:].rearrange("p b (j c i) -> p b c j i", j=4, c=16, i=4)
        nc.vector.tensor_copy(out=dst1[:, 0:4], in_=src1[:, 0:4])
        nc.scalar.copy(out=dst1[:, 6:8], in_=src1[:, 6:8])

        k_sp = const.tile([PAIRS, 2], F32, name="k_sp")
        nc.vector.scalar_tensor_tensor(
            out=k_sp[:], in0=k_w[:], scalar=2.0, in1=k_rl[:], op0=ALU.mult, op1=ALU.add
        )
        rk = const.tile([PAIRS, 2], F32, name="rk")
        nc.vector.reciprocal(out=rk[:], in_=k_sp[:])
        raw_v = raw[:].rearrange("h g l (c e) -> h e g l c", e=2)
        scaled_v = scaled[0:PAIRS].rearrange("h e g (l c) -> h e g l c", l=2)
        for ml in range(2):
            for nl in range(2):
                nc.scalar.activation(out=scaled_v[:, ml, :, nl, :], in_=raw_v[:, ml, :, nl, :], func=ACT.Copy,
                                     scale=rk[:, nl : nl + 1])
        nc.vector.tensor_copy(out=dst1[:, 4:6], in_=src1[:, 4:6])
        nc.vector.tensor_copy(out=t_perm[:], in_=t_ps[:].rearrange("q (p u e) -> q u p e", u=2, e=2))
        x_regroup(2, False)
        x_regroup_rest(2)
        x_quant(1, False)
        tabs = []
        for ml in range(2):
            tab_ps = ps_a.tile([P, 3, P], F32, name="tab_ps", tag="at")
            for g in range(3):
                nc.tensor.transpose(tab_ps[:, g, :], scaled[:, ml, g, :], ident[:])
            tabs.append((tab_ps, const.tile([P, 2, PAIRS], F32, name="tp%d" % ml),
                         const.tile([P, 2, PAIRS], F32, name="tn%d" % ml)))

        def tables(ml):
            tab_ps, tp, tn = tabs[ml]
            nc.scalar.copy(out=tp[:], in_=tab_ps[:, 0:2, 0:PAIRS])
            nc.scalar.activation(out=tn[:], in_=tab_ps[:, 1:3, 0:PAIRS], func=ACT.Copy, scale=-1.0)

        def sigmoids(i):
            h, ml = divmod(i, 2)
            if h == 0:
                tables(ml)
            tab_ps, tp, tn = tabs[ml]
            s1, s2 = s_pairs[i % SIG_PAIRS]
            nc.scalar.activation(out=s1[:, 0:L], in_=t_flat, func=ACT.Sigmoid,
                                 scale=tn[:, 0, h : h + 1], bias=tp[:, 0, h : h + 1])
            nc.scalar.activation(out=s2[:, 0:L], in_=t_flat, func=ACT.Sigmoid,
                                 scale=tp[:, 1, h : h + 1], bias=tn[:, 1, h : h + 1])

        def product(i):
            g, c = divmod(i, 4)
            if c == 0:
                den = small.tile([P, 4], F32, name="den")
                den_tiles[g] = den
            s1, s2 = s_pairs[i % SIG_PAIRS]
            a16 = apool.tile([P, L + 2], BF16, name="a16", align_bytes=64)
            nc.vector.scalar_tensor_tensor(
                out=a16[:, 0 : L + 1], in0=s1[:, 0 : L + 1], scalar=1.0, in1=s2[:, 0 : L + 1],
                op0=ALU.mult, op1=ALU.mult, accum_out=den_tiles[g][:, c : c + 1],
            )
            a16_tiles[i] = a16

        def reciprocal(g):
            rec = small.tile([P, 4], F32, name="rec")
            nc.vector.reciprocal(out=rec[:], in_=den_tiles[g][:])
            rec_tiles[g] = rec

        def transposes(i):
            words = a16_tiles[i][:, 0:L].bitcast(F32)
            at = ps_a.tile([P, 2, P], F32, name="at", tag="at")
            for u in range(2):
                nc.tensor.transpose(at[:, u, :], words[:, u * P : (u + 1) * P], swp[:])
            at_tiles[i] = at

        def alpha_out(i):
            a_in = apool.tile([P, P, 4], BF16, name="a_in", align_bytes=64)
            nc.scalar.copy(
                out=a_in[:].rearrange("p q j -> p (q j)").bitcast(F32),
                in_=at_tiles[i][:].rearrange("p u q -> p q u"),
            )
            ain_tiles[i] = a_in

        def alpha_quant(i):
            a_in = ain_tiles[i]
            s = i % A_SLOTS
            nc.vector.quantize_mx(
                out=a_cod[s][:, 64:192].bitcast(FP8X4),
                scales=a_pl[s][:, 64:192],
                in_=a_in[:].rearrange("p q j -> p (q j)"),
            )

        def passes(i):
            h = i // 2
            s = i % A_SLOTS
            acc = ps_o.tile([P, B * F], F32, name="acc")
            for nl in range(2):
                xc, xp = xq_tiles[2 * h + nl]
                nc.tensor.matmul_mx(
                    out=acc[:],
                    lhsT=a_cod[s][:, 128 - 128 * nl : 256 - 128 * nl].bitcast(FP8X4),
                    lhsT_scale=a_pl[s][:, 128 - 128 * nl : 256 - 128 * nl],
                    rhs=xc[:].bitcast(FP8X4),
                    rhs_scale=xp[:],
                    start=(nl == 0),
                    stop=(nl == 1),
                )
            acc_tiles[i] = acc

        def store(h, bs):
            nc.sync.dma_start(
                out=ov[h][:, bs, :], in_=osb_tiles[h][:, bs, :, :].rearrange("q b e f -> q b (e f)")
            )

        def result_out(i):
            h, ml = divmod(i, 2)
            if ml == 0:
                osb = opool.tile([P, B, 2, F], F32, name="osb")
                osb_tiles[h] = osb
            nc.scalar.activation(
                out=osb_tiles[h][:, :, ml, :],
                in_=acc_tiles[i][:].rearrange("q (b f) -> q b f", b=B),
                func=ACT.Copy,
                scale=rec_tiles[i // 4][:, i % 4 : i % 4 + 1],
            )
            if ml == 1:
                store(h, slice(0, 4))
                store(h, slice(4, 8))

        def last_pair():
            h = PAIRS - 1
            osb = opool.tile([P, B, 2, F], F32, name="osb")
            osb_tiles[h] = osb
            rec = rec_tiles[(TILES - 1) // 4]
            for k in range(4):
                cols = slice(128 * k, 128 * k + 128)
                accs = []
                for ml in range(2):
                    s = (2 * h + ml) % A_SLOTS
                    acc = ps_o.tile([P, 2 * F], F32, name="acc")
                    accs.append(acc)
                    for nl in range(2):
                        xc, xp = xq_tiles[2 * h + nl]
                        nc.tensor.matmul_mx(
                            out=acc[:],
                            lhsT=a_cod[s][:, 128 - 128 * nl : 256 - 128 * nl].bitcast(FP8X4),
                            lhsT_scale=a_pl[s][:, 128 - 128 * nl : 256 - 128 * nl],
                            rhs=xc[:, cols].bitcast(FP8X4),
                            rhs_scale=xp[:, cols],
                            start=(nl == 0),
                            stop=(nl == 1),
                        )
                bs = slice(2 * k, 2 * k + 2)
                nc.scalar.activation(
                    out=osb[:, bs, 0, :], in_=accs[0][:].rearrange("q (b f) -> q b f", b=2),
                    func=ACT.Copy, scale=rec[:, 2:3],
                )
                nc.vector.tensor_scalar_mul(
                    out=osb[:, bs, 1, :], in0=accs[1][:].rearrange("q (b f) -> q b f", b=2),
                    scalar1=rec[:, 3:4],
                )
                store(h, bs)

        next_x = 3
        next_load = PRELOAD
        pending = [2]
        for s in range(TILES + 4):
            ahead = next_x + 1 if s not in X_SKIP else next_x
            if s + 1 not in X_SKIP and ahead < N and spread(ahead):
                x_spread(ahead)
            if s < TILES:
                sigmoids(s)
            if 0 <= s - 1 < TILES:
                product(s - 1)
                transposes(s - 1)
            fresh = []
            if s not in X_SKIP and next_x < N:
                x_regroup(next_x, next_x == N - 1)
                fresh.append(next_x)
                next_x += 1
            if 0 <= s - 3 < TILES:
                alpha_quant(s - 3)
            if 0 <= s - 1 < TILES and (s - 1) % 4 == 3:
                reciprocal((s - 1) // 4)
            for n in pending:
                x_quant(n, n == N - 1)
            pending = fresh
            for n in fresh:
                if shared(n):
                    x_regroup_rest(n)
            if 0 <= s - 2 < TILES:
                alpha_out(s - 2)
            if 0 <= s - 4 < TILES - 2:
                passes(s - 4)
            if 0 <= s - 5 < TILES - 2:
                result_out(s - 5)
            if next_load < N:
                load_x(next_load)
                next_load += 1
        last_pair()
